import numpy as np
import ml_dtypes


def mxq(x, axis, fmt="e4m3"):
    dtype, down = {"e4m3": (ml_dtypes.float8_e4m3fn, 7), "e5m2": (ml_dtypes.float8_e5m2, 14)}[fmt]
    v = np.moveaxis(np.asarray(x, np.float32).astype(ml_dtypes.bfloat16).astype(np.float64), axis, -1)
    blocks = v.reshape(v.shape[:-1] + (-1, 32))
    amax = np.abs(blocks).max(-1, keepdims=True)
    byte = np.maximum(np.where(amax > 0, np.frexp(amax)[1] - 1 + 127, 0) - down, 1)
    scale = np.exp2(byte - 127.0)
    codes = (blocks / scale).astype(np.float32).astype(dtype).astype(np.float64)
    return np.moveaxis((codes * scale).reshape(v.shape), -1, axis)


WIDE = False


def mx_kscale(k):
    if not WIDE:
        return np.ones(k)
    levels = np.array([10, -10, 5, -5, 0])
    a = np.random.permutation(np.resize(levels, k // 512 * 4)).reshape(k // 512, 4)
    idx = np.arange(k)
    return np.exp2(a[idx // 512, idx % 128 // 32])


BF16 = ml_dtypes.bfloat16


def bf(x):
    return np.asarray(x, np.float32).astype(BF16)


def f64(x):
    return np.asarray(x).astype(np.float64)


B, C, CP, L = 1, 1024, 512, 1024
EPS = 1e-6


def setup_inputs():
    t = mx_kscale(CP)
    mask = 0.1 + 0.9 * np.random.random((B, 1, L))
    return {"q": bf(np.random.standard_normal((B, CP, L)) * 1.5),
            "k": bf(np.random.standard_normal((B, CP, L)) * 1.5),
            "v": bf(np.random.standard_normal((B, CP, L)) * 1.5 * t[None, :, None]),
            "mask": bf(mask),
            "wo": bf(np.random.standard_normal((C, CP)) * 2.0 / np.sqrt(CP) / t[None, :]),
            "bo": bf(np.random.standard_normal(C) * 0.3)}


def reference(q, k, v, mask, wo, bo):
    pm = f64(mask)[:, 0:1, :]
    energy = f64(q).transpose(0, 2, 1) @ f64(k) * (1.0 / np.sqrt(CP))
    z = energy + np.log(pm + EPS)
    e = np.exp(z - z.max(-1, keepdims=True))
    p = e * pm
    o = (mxq(f64(v), 2, "e4m3") @ mxq(p, 2, "e4m3").transpose(0, 2, 1)) / e.sum(-1)[:, None, :]
    h = np.maximum(o, 0.0)
    y = (mxq(f64(wo), 1, "e4m3") @ mxq(h, 1, "e4m3")) + f64(bo)[None, :, None]
    return y * pm

@@ -1,0 +1,286 @@
+import math
+from contextlib import ExitStack
+
+import concourse.mybir as mybir
+from concourse.masks import make_identity
+
+F32 = mybir.dt.float32
+BF16 = mybir.dt.bfloat16
+U32 = mybir.dt.uint32
+U8 = mybir.dt.uint8
+FP8X4 = mybir.dt.float8_e4m3fn_x4
+ALU = mybir.AluOpType
+ACT = mybir.ActivationFunctionType
+
+P = 128
+PACK = 4
+K_PASS = P * PACK
+BANK = 512
+CP = 512
+L = 1024
+C = 1024
+EPS = 1e-6
+
+C_TILES = CP // P
+L_TILES = L // P
+J_TILES = C // P
+KEY_PASSES = L // K_PASS
+L_BLOCK = 256
+J_PER_STEP = 4
+
+FLOPS = 2 * L * L * CP + 2 * CP * L * L + 2 * C * CP * L
+
+
+def tile_attlayer_pa_kernel(tc, q, k, v, mask, wo, bo, out):
+    nc = tc.nc
+    with ExitStack() as ctx:
+        keep = ctx.enter_context(tc.tile_pool(name="keep", bufs=1))
+        work = ctx.enter_context(tc.tile_pool(name="work", bufs=3))
+        stats = ctx.enter_context(tc.tile_pool(name="stats", bufs=4))
+        store = ctx.enter_context(tc.tile_pool(name="store", bufs=4))
+        psum_energy = ctx.enter_context(tc.psum_pool(name="psum_energy", bufs=4))
+        psum_turn = ctx.enter_context(tc.psum_pool(name="psum_turn", bufs=2))
+        psum_mx = ctx.enter_context(tc.psum_pool(name="psum_mx", bufs=2))
+
+        mask_rows = keep.tile([P, L], BF16)
+        nc.vector.memset(mask_rows[:], 0.0)
+        nc.scalar.dma_start(out=mask_rows[0:1, :], in_=mask[0])
+        bo_rows = keep.tile([P, P], BF16)
+        nc.vector.memset(bo_rows[:], 0.0)
+        nc.scalar.dma_start(out=bo_rows[0:J_TILES, :], in_=bo.rearrange("(t p) -> t p", p=P))
+
+        k_sb = keep.tile([P, C_TILES, L], BF16)
+        q_sb = keep.tile([P, C_TILES, L], BF16)
+        for ct in range(C_TILES):
+            rows = slice(ct * P, (ct + 1) * P)
+            nc.sync.dma_start(out=k_sb[:, ct, :], in_=k[0, rows, :])
+            nc.sync.dma_start(out=q_sb[:, ct, :], in_=q[0, rows, :])
+        v_sb = keep.tile([P, C_TILES, L], BF16)
+        nc.sync.dma_start(out=v_sb[:], in_=v[0].rearrange("(t p) m -> p t m", p=P))
+        wo_sb = keep.tile([P, J_TILES, CP], BF16)
+        nc.sync.dma_start(out=wo_sb[:], in_=wo.rearrange("(t p) c -> p t c", p=P))
+
+        ones = keep.tile([P, P], BF16)
+        nc.vector.memset(ones[:], 1.0)
+        eps = keep.tile([P, 1], F32)
+        nc.vector.memset(eps[:], EPS)
+        ident_bf16 = keep.tile([P, P], BF16)
+        make_identity(nc, ident_bf16[:])
+        ident_f32 = keep.tile([P, P], F32)
+        make_identity(nc, ident_f32[:])
+
+        mask_queries = keep.tile([P, L], F32)
+        mask_keys = keep.tile([P, L], F32)
+        log_mask_keys = keep.tile([P, L], F32)
+        for g in range(KEY_PASSES):
+            cols = slice(g * BANK, (g + 1) * BANK)
+            spread = psum_mx.tile([P, BANK], F32, tag="mx")
+            nc.tensor.matmul(out=spread[:], lhsT=ones[:], rhs=mask_rows[:, cols], start=True, stop=True)
+            in_key_order = spread[:].rearrange("p (w e) -> p e w", e=2)
+            nc.scalar.activation(
+                out=log_mask_keys[:, cols].rearrange("p (e w) -> p e w", e=2),
+                in_=in_key_order,
+                func=ACT.Ln,
+                bias=eps[:, 0:1],
+                scale=1.0,
+            )
+            nc.vector.tensor_copy(out=mask_keys[:, cols].rearrange("p (e w) -> p e w", e=2), in_=in_key_order)
+            nc.vector.tensor_copy(out=mask_queries[:, cols], in_=spread[:])
+
+        v_codes = keep.tile([P, KEY_PASSES, CP], U32, align_bytes=64)
+        v_scales = keep.tile([P, KEY_PASSES, CP], U8, align_bytes=64)
+        wo_codes = keep.tile([P, C], U32, align_bytes=64)
+        wo_scales = keep.tile([P, C], U8, align_bytes=64)
+        h_codes = keep.tile([P, L], U32, align_bytes=64)
+        h_scales = keep.tile([P, L], U8, align_bytes=64)
+        bo_col = keep.tile([P, J_TILES], F32)
+
+        energy_banks = {}
+        weights = {}
+        row_sums = {}
+        weight_codes = {}
+        hidden = {}
+
+        def energy(query_tiles):
+            for i in query_tiles:
+                for g in range(KEY_PASSES):
+                    bank = psum_energy.tile([P, BANK], F32, tag="energy")
+                    energy_banks[(i, g)] = bank
+            for ct in range(C_TILES):
+                for i in query_tiles:
+                    for g in range(KEY_PASSES):
+                        nc.tensor.matmul(
+                            out=energy_banks[(i, g)][:].rearrange("p (e w) -> p e w", e=2),
+                            lhsT=q_sb[:, ct, i * P : (i + 1) * P],
+                            rhs=k_sb[:, ct, g * BANK : (g + 1) * BANK].rearrange("p (w e) -> p e w", e=2),
+                            start=(ct == 0),
+                            stop=(ct == C_TILES - 1),
+                        )
+
+        def softmax(i):
+            z = work.tile([P, L], F32)
+            for g in range(KEY_PASSES):
+                cols = slice(g * BANK, (g + 1) * BANK)
+                nc.vector.scalar_tensor_tensor(
+                    out=z[:, cols],
+                    in0=energy_banks[(i, g)][:],
+                    scalar=1.0 / math.sqrt(CP),
+                    in1=log_mask_keys[:, cols],
+                    op0=ALU.mult,
+                    op1=ALU.add,
+                )
+            neg_max = stats.tile([P, 1], F32)
+            nc.vector.tensor_reduce(out=neg_max[:], in_=z[:], axis=mybir.AxisListType.X, op=ALU.max, negate=True)
+            exp_z = work.tile([P, L], F32)
+            row_sum = stats.tile([P, 1], F32)
+            nc.scalar.activation(
+                out=exp_z[:], in_=z[:], func=ACT.Exp, bias=neg_max[:, 0:1], scale=1.0, accum_out=row_sum[:, 0:1]
+            )
+            row_sums[i] = row_sum
+            p = work.tile([P, L], BF16)
+            nc.gpsimd.tensor_tensor(out=p[:], in0=exp_z[:], in1=mask_keys[:], op=ALU.mult)
+            weights[i] = p
+
+        def turn_weights(i):
+            turned = psum_turn.tile([P, KEY_PASSES, PACK, P], BF16, tag="turn")
+            for g in range(KEY_PASSES):
+                for u in range(2):
+                    for e in range(2):
+                        first = g * K_PASS + e * 2 * P + u * P
+                        nc.tensor.transpose(turned[:, g, 2 * u + e, :], weights[i][:, first : first + P], ident_bf16[:])
+            grouped = work.tile([P, KEY_PASSES, P, PACK], BF16, align_bytes=64, tag="grouped_p")
+            nc.scalar.copy(out=grouped[:], in_=turned[:].rearrange("p g t r -> p g r t"))
+            codes = work.tile([P, KEY_PASSES, P], U32, align_bytes=64, tag="p_codes")
+            scales = work.tile([P, KEY_PASSES, P], U8, align_bytes=64, tag="p_scales")
+            nc.vector.quantize_mx(
+                out=codes[:].rearrange("p g r -> p (g r)").bitcast(FP8X4),
+                scales=scales[:].rearrange("p g r -> p (g r)"),
+                in_=grouped[:].rearrange("p g r t -> p (g r t)"),
+            )
+            weight_codes[i] = (codes, scales)
+
+        def attend(i):
+            codes, scales = weight_codes[i]
+            attended = psum_mx.tile([P, CP], F32, tag="mx")
+            for g in range(KEY_PASSES):
+                nc.tensor.matmul_mx(
+                    out=attended[:],
+                    lhsT=codes[:, g, :].bitcast(FP8X4),
+                    lhsT_scale=scales[:, g, :],
+                    rhs=v_codes[:, g, :].bitcast(FP8X4),
+                    rhs_scale=v_scales[:, g, :],
+                    start=(g == 0),
+                    stop=(g == KEY_PASSES - 1),
+                )
+            inv_sum = stats.tile([P, 1], F32)
+            nc.vector.reciprocal(out=inv_sum[:], in_=row_sums[i][:])
+            h = work.tile([P, CP], BF16)
+            nc.scalar.activation(out=h[:], in_=attended[:], func=ACT.Relu, scale=inv_sum[:, 0:1])
+            hidden[i] = h
+
+        def turn_hidden(i):
+            turned = psum_turn.tile([P, PACK, P], BF16, tag="turn")
+            for t in range(PACK):
+                nc.tensor.transpose(turned[:, t, :], hidden[i][:, t * P : (t + 1) * P], ident_bf16[:])
+            grouped = work.tile([P, P, PACK], BF16, align_bytes=64, tag="grouped_h")
+            nc.scalar.copy(out=grouped[:], in_=turned[:].rearrange("p t r -> p r t"))
+            cols = slice(i * P, (i + 1) * P)
+            nc.vector.quantize_mx(
+                out=h_codes[:, cols].bitcast(FP8X4),
+                scales=h_scales[:, cols],
+                in_=grouped[:].rearrange("p r t -> p (r t)"),
+            )
+
+        def project(block, j_tiles):
+            cols = slice(block * L_BLOCK, (block + 1) * L_BLOCK)
+            for jt in j_tiles:
+                rows = slice(jt * P, (jt + 1) * P)
+                projected = psum_mx.tile([P, L_BLOCK], F32, tag="mx")
+                nc.tensor.matmul_mx(
+                    out=projected[:],
+                    lhsT=wo_codes[:, rows].bitcast(FP8X4),
+                    lhsT_scale=wo_scales[:, rows],
+                    rhs=h_codes[:, cols].bitcast(FP8X4),
+                    rhs_scale=h_scales[:, cols],
+                    start=True,
+                    stop=True,
+                )
+                result = store.tile([P, L_BLOCK], F32)
+                nc.vector.scalar_tensor_tensor(
+                    out=result[:],
+                    in0=projected[:],
+                    scalar=bo_col[:, jt : jt + 1],
+                    in1=mask_queries[:, cols],
+                    op0=ALU.add,
+                    op1=ALU.mult,
+                )
+                nc.sync.dma_start(out=out[0, rows, cols], in_=result[:])
+
+        def prepare_v(g, half):
+            words = v_sb[:].bitcast(F32)
+            turned = psum_turn.tile([P, 2, 2 * P], F32, tag="turn")
+            for u in range(2):
+                for s in range(2):
+                    first = g * 2 * P + u * P
+                    nc.tensor.transpose(
+                        turned[:, u, s * P : (s + 1) * P], words[:, 2 * half + s, first : first + P], ident_f32[:]
+                    )
+            grouped = work.tile([P, 2 * P, PACK], BF16, align_bytes=64, tag="grouped_w")
+            nc.scalar.copy(
+                out=grouped[:].bitcast(F32).rearrange("p (e r) u -> p e r u", e=2),
+                in_=turned[:].rearrange("p u (r e) -> p e r u", e=2),
+            )
+            cols = slice(half * 2 * P, (half + 1) * 2 * P)
+            nc.vector.quantize_mx(
+                out=v_codes[:, g, cols].bitcast(FP8X4),
+                scales=v_scales[:, g, cols],
+                in_=grouped[:].rearrange("p n t -> p (n t)"),
+            )
+
+        def prepare_wo(pair):
+            words = wo_sb[:].bitcast(F32)
+            turned = psum_turn.tile([P, 2, 2 * P], F32, tag="turn")
+            for u in range(2):
+                for s in range(2):
+                    nc.tensor.transpose(
+                        turned[:, u, s * P : (s + 1) * P], words[:, 2 * pair + s, u * P : (u + 1) * P], ident_f32[:]
+                    )
+            grouped = work.tile([P, 2 * P, PACK], BF16, align_bytes=64, tag="grouped_w")
+            nc.vector.tensor_copy(out=grouped[:].bitcast(F32), in_=turned[:].rearrange("p u j -> p j u"))
+            cols = slice(pair * 2 * P, (pair + 1) * 2 * P)
+            nc.vector.quantize_mx(
+                out=wo_codes[:, cols].bitcast(FP8X4),
+                scales=wo_scales[:, cols],
+                in_=grouped[:].rearrange("p n t -> p (n t)"),
+            )
+
+        def prepare_bias():
+            turned = psum_turn.tile([P, P], BF16, tag="turn")
+            nc.tensor.transpose(turned[:], bo_rows[:], ident_bf16[:])
+            nc.vector.tensor_copy(out=bo_col[:], in_=turned[:, 0:J_TILES])
+
+        first_project = 5
+        steps = first_project + (L // L_BLOCK) * (J_TILES // J_PER_STEP)
+        energy([0, 1])
+        for step in range(steps):
+            if step < L_TILES:
+                softmax(step)
+            if step + 2 < L_TILES:
+                energy([step + 2])
+            if 0 <= step - 2 < L_TILES:
+                attend(step - 2)
+            if step >= first_project:
+                block, part = divmod(step - first_project, J_TILES // J_PER_STEP)
+                project(block, range(part * J_PER_STEP, (part + 1) * J_PER_STEP))
+            if step < 2:
+                prepare_v(step, 0)
+                prepare_v(step, 1)
+            elif step < 4:
+                prepare_wo(2 * (step - 2))
+                prepare_wo(2 * (step - 2) + 1)
+            elif step == 4:
+                prepare_bias()
+            if 0 <= step - 3 < L_TILES:
+                turn_hidden(step - 3)
+            if 0 <= step - 1 < L_TILES:
+                turn_weights(step - 1)

@@ -26,7 +26,28 @@ L_TILES = L // P
 J_TILES = C // P
 KEY_PASSES = L // K_PASS
 L_BLOCK = 256
-J_PER_STEP = 4
+TILES_PER_BLOCK = L_BLOCK // P
+J_PER_STEP = J_TILES // TILES_PER_BLOCK
+V_PIECES = 4
+WO_PIECES = 4
+
+CHAIN = [
+    "energy",
+    "scores",
+    "exponentials",
+    "weigh",
+    "turn_weights",
+    "group_weights",
+    "quantise_weights",
+    "attend",
+    "hidden",
+    "turn_hidden",
+    "group_hidden",
+    "quantise_hidden",
+    "project",
+    "finish",
+]
+FIRST_PIECE_STEP = 2
 
 FLOPS = 2 * L * L * CP + 2 * CP * L * L + 2 * C * CP * L
 
@@ -35,9 +56,9 @@ def tile_attlayer_pa_kernel(tc, q, k, v, mask, wo, bo, out):
     nc = tc.nc
     with ExitStack() as ctx:
         keep = ctx.enter_context(tc.tile_pool(name="keep", bufs=1))
-        work = ctx.enter_context(tc.tile_pool(name="work", bufs=3))
-        stats = ctx.enter_context(tc.tile_pool(name="stats", bufs=4))
-        store = ctx.enter_context(tc.tile_pool(name="store", bufs=4))
+        work = ctx.enter_context(tc.tile_pool(name="work", bufs=4))
+        stats = ctx.enter_context(tc.tile_pool(name="stats", bufs=8))
+        store = ctx.enter_context(tc.tile_pool(name="store", bufs=8))
         psum_energy = ctx.enter_context(tc.psum_pool(name="psum_energy", bufs=4))
         psum_turn = ctx.enter_context(tc.psum_pool(name="psum_turn", bufs=2))
         psum_mx = ctx.enter_context(tc.psum_pool(name="psum_mx", bufs=2))
@@ -49,12 +70,20 @@ def tile_attlayer_pa_kernel(tc, q, k, v, mask, wo, bo, out):
         nc.vector.memset(bo_rows[:], 0.0)
         nc.scalar.dma_start(out=bo_rows[0:J_TILES, :], in_=bo.rearrange("(t p) -> t p", p=P))
 
-        k_sb = keep.tile([P, C_TILES, L], BF16)
-        q_sb = keep.tile([P, C_TILES, L], BF16)
-        for ct in range(C_TILES):
-            rows = slice(ct * P, (ct + 1) * P)
-            nc.sync.dma_start(out=k_sb[:, ct, :], in_=k[0, rows, :])
-            nc.sync.dma_start(out=q_sb[:, ct, :], in_=q[0, rows, :])
+        k_view = k[0].rearrange("(t p) m -> p t m", p=P)
+        q_view = q[0].rearrange("(t p) l -> p t l", p=P)
+        q_first = keep.tile([P, C_TILES, P], BF16)
+        nc.sync.dma_start(out=q_first[:], in_=q_view[:, :, 0:P])
+        k_halves = {}
+        for g in range(KEY_PASSES):
+            k_half = keep.tile([P, C_TILES, BANK], BF16, name="k_half%d" % g)
+            nc.sync.dma_start(out=k_half[:], in_=k_view[:, :, g * BANK : (g + 1) * BANK])
+            k_halves[g] = k_half
+        q_rest = keep.tile([P, C_TILES, L - P], BF16)
+        nc.sync.dma_start(out=q_rest[:], in_=q_view[:, :, P:L])
+        queries = {0: q_first[:]}
+        for i in range(1, L_TILES):
+            queries[i] = q_rest[:, :, (i - 1) * P : i * P]
         v_sb = keep.tile([P, C_TILES, L], BF16)
         nc.sync.dma_start(out=v_sb[:], in_=v[0].rearrange("(t p) m -> p t m", p=P))
         wo_sb = keep.tile([P, J_TILES, CP], BF16)
@@ -87,6 +116,9 @@ def tile_attlayer_pa_kernel(tc, q, k, v, mask, wo, bo, out):
             nc.vector.tensor_copy(out=mask_keys[:, cols].rearrange("p (e w) -> p e w", e=2), in_=in_key_order)
             nc.vector.tensor_copy(out=mask_queries[:, cols], in_=spread[:])
 
+        table_change = keep.tile([P, 1], F32)
+        nc.scalar.activation(out=table_change[:], in_=log_mask_keys[:, L - 1 : L], func=ACT.Exp)
+
         v_codes = keep.tile([P, KEY_PASSES, CP], U32, align_bytes=64)
         v_scales = keep.tile([P, KEY_PASSES, CP], U8, align_bytes=64)
         wo_codes = keep.tile([P, C], U32, align_bytes=64)
@@ -96,28 +128,35 @@ def tile_attlayer_pa_kernel(tc, q, k, v, mask, wo, bo, out):
         bo_col = keep.tile([P, J_TILES], F32)
 
         energy_banks = {}
-        weights = {}
+        shifted = {}
+        exponents = {}
         row_sums = {}
+        weights = {}
+        turned_weights = {}
+        grouped_weights = {}
         weight_codes = {}
-        hidden = {}
+        attended = {}
+        hidden_tiles = {}
+        turned_hidden = {}
+        grouped_hidden = {}
+        turned_pieces = {}
+        grouped_pieces = {}
+        projected = {}
 
-        def energy(query_tiles):
-            for i in query_tiles:
-                for g in range(KEY_PASSES):
-                    bank = psum_energy.tile([P, BANK], F32, tag="energy")
-                    energy_banks[(i, g)] = bank
-            for ct in range(C_TILES):
-                for i in query_tiles:
-                    for g in range(KEY_PASSES):
-                        nc.tensor.matmul(
-                            out=energy_banks[(i, g)][:].rearrange("p (e w) -> p e w", e=2),
-                            lhsT=q_sb[:, ct, i * P : (i + 1) * P],
-                            rhs=k_sb[:, ct, g * BANK : (g + 1) * BANK].rearrange("p (w e) -> p e w", e=2),
-                            start=(ct == 0),
-                            stop=(ct == C_TILES - 1),
-                        )
+        def energy(i):
+            for g in range(KEY_PASSES):
+                bank = psum_energy.tile([P, BANK], F32, tag="energy")
+                for ct in range(C_TILES):
+                    nc.tensor.matmul(
+                        out=bank[:].rearrange("p (e w) -> p e w", e=2),
+                        lhsT=queries[i][:, ct, :],
+                        rhs=k_halves[g][:, ct, :].rearrange("p (w e) -> p e w", e=2),
+                        start=(ct == 0),
+                        stop=(ct == C_TILES - 1),
+                    )
+                energy_banks[(i, g)] = bank
 
-        def softmax(i):
+        def scores(i):
             z = work.tile([P, L], F32)
             for g in range(KEY_PASSES):
                 cols = slice(g * BANK, (g + 1) * BANK)
@@ -131,14 +170,21 @@ def tile_attlayer_pa_kernel(tc, q, k, v, mask, wo, bo, out):
                 )
             neg_max = stats.tile([P, 1], F32)
             nc.vector.tensor_reduce(out=neg_max[:], in_=z[:], axis=mybir.AxisListType.X, op=ALU.max, negate=True)
+            shifted[i] = (z, neg_max)
+
+        def exponentials(i):
+            z, neg_max = shifted[i]
             exp_z = work.tile([P, L], F32)
             row_sum = stats.tile([P, 1], F32)
             nc.scalar.activation(
                 out=exp_z[:], in_=z[:], func=ACT.Exp, bias=neg_max[:, 0:1], scale=1.0, accum_out=row_sum[:, 0:1]
             )
+            exponents[i] = exp_z
             row_sums[i] = row_sum
+
+        def weigh(i):
             p = work.tile([P, L], BF16)
-            nc.gpsimd.tensor_tensor(out=p[:], in0=exp_z[:], in1=mask_keys[:], op=ALU.mult)
+            nc.gpsimd.tensor_tensor(out=p[:], in0=exponents[i][:], in1=mask_keys[:], op=ALU.mult)
             weights[i] = p
 
         def turn_weights(i):
@@ -148,23 +194,33 @@ def tile_attlayer_pa_kernel(tc, q, k, v, mask, wo, bo, out):
                     for e in range(2):
                         first = g * K_PASS + e * 2 * P + u * P
                         nc.tensor.transpose(turned[:, g, 2 * u + e, :], weights[i][:, first : first + P], ident_bf16[:])
+            turned_weights[i] = turned
+
+        def group_weights(i):
             grouped = work.tile([P, KEY_PASSES, P, PACK], BF16, align_bytes=64, tag="grouped_p")
-            nc.scalar.copy(out=grouped[:], in_=turned[:].rearrange("p g t r -> p g r t"))
+            values_last = turned_weights[i][:].rearrange("p g t r -> p g r t")
+            if i < L_TILES // 2:
+                nc.scalar.copy(out=grouped[:], in_=values_last)
+            else:
+                nc.vector.tensor_copy(out=grouped[:], in_=values_last)
+            grouped_weights[i] = grouped
+
+        def quantise_weights(i):
             codes = work.tile([P, KEY_PASSES, P], U32, align_bytes=64, tag="p_codes")
             scales = work.tile([P, KEY_PASSES, P], U8, align_bytes=64, tag="p_scales")
             nc.vector.quantize_mx(
                 out=codes[:].rearrange("p g r -> p (g r)").bitcast(FP8X4),
                 scales=scales[:].rearrange("p g r -> p (g r)"),
-                in_=grouped[:].rearrange("p g r t -> p (g r t)"),
+                in_=grouped_weights[i][:].rearrange("p g r t -> p (g r t)"),
             )
             weight_codes[i] = (codes, scales)
 
         def attend(i):
             codes, scales = weight_codes[i]
-            attended = psum_mx.tile([P, CP], F32, tag="mx")
+            bank = psum_mx.tile([P, CP], F32, tag="mx")
             for g in range(KEY_PASSES):
                 nc.tensor.matmul_mx(
-                    out=attended[:],
+                    out=bank[:],
                     lhsT=codes[:, g, :].bitcast(FP8X4),
                     lhsT_scale=scales[:, g, :],
                     rhs=v_codes[:, g, :].bitcast(FP8X4),
@@ -174,113 +230,148 @@ def tile_attlayer_pa_kernel(tc, q, k, v, mask, wo, bo, out):
                 )
             inv_sum = stats.tile([P, 1], F32)
             nc.vector.reciprocal(out=inv_sum[:], in_=row_sums[i][:])
+            attended[i] = (bank, inv_sum)
+
+        def hidden(i):
+            bank, inv_sum = attended[i]
             h = work.tile([P, CP], BF16)
-            nc.scalar.activation(out=h[:], in_=attended[:], func=ACT.Relu, scale=inv_sum[:, 0:1])
-            hidden[i] = h
+            nc.scalar.activation(out=h[:], in_=bank[:], func=ACT.Relu, scale=inv_sum[:, 0:1])
+            hidden_tiles[i] = h
 
         def turn_hidden(i):
             turned = psum_turn.tile([P, PACK, P], BF16, tag="turn")
             for t in range(PACK):
-                nc.tensor.transpose(turned[:, t, :], hidden[i][:, t * P : (t + 1) * P], ident_bf16[:])
+                nc.tensor.transpose(turned[:, t, :], hidden_tiles[i][:, t * P : (t + 1) * P], ident_bf16[:])
+            turned_hidden[i] = turned
+
+        def group_hidden(i):
             grouped = work.tile([P, P, PACK], BF16, align_bytes=64, tag="grouped_h")
-            nc.scalar.copy(out=grouped[:], in_=turned[:].rearrange("p t r -> p r t"))
+            nc.scalar.copy(out=grouped[:], in_=turned_hidden[i][:].rearrange("p t r -> p r t"))
+            grouped_hidden[i] = grouped
+
+        def quantise_hidden(i):
             cols = slice(i * P, (i + 1) * P)
             nc.vector.quantize_mx(
                 out=h_codes[:, cols].bitcast(FP8X4),
                 scales=h_scales[:, cols],
-                in_=grouped[:].rearrange("p r t -> p (r t)"),
+                in_=grouped_hidden[i][:].rearrange("p r t -> p (r t)"),
             )
 
-        def project(block, j_tiles):
+        def project(block, jt):
+            bank = psum_energy.tile([P, L_BLOCK], F32, tag="energy")
+            rows = slice(jt * P, (jt + 1) * P)
             cols = slice(block * L_BLOCK, (block + 1) * L_BLOCK)
-            for jt in j_tiles:
-                rows = slice(jt * P, (jt + 1) * P)
-                projected = psum_mx.tile([P, L_BLOCK], F32, tag="mx")
-                nc.tensor.matmul_mx(
-                    out=projected[:],
-                    lhsT=wo_codes[:, rows].bitcast(FP8X4),
-                    lhsT_scale=wo_scales[:, rows],
-                    rhs=h_codes[:, cols].bitcast(FP8X4),
-                    rhs_scale=h_scales[:, cols],
-                    start=True,
-                    stop=True,
-                )
-                result = store.tile([P, L_BLOCK], F32)
-                nc.vector.scalar_tensor_tensor(
-                    out=result[:],
-                    in0=projected[:],
-                    scalar=bo_col[:, jt : jt + 1],
-                    in1=mask_queries[:, cols],
-                    op0=ALU.add,
-                    op1=ALU.mult,
-                )
-                nc.sync.dma_start(out=out[0, rows, cols], in_=result[:])
+            nc.tensor.matmul_mx(
+                out=bank[:],
+                lhsT=wo_codes[:, rows].bitcast(FP8X4),
+                lhsT_scale=wo_scales[:, rows],
+                rhs=h_codes[:, cols].bitcast(FP8X4),
+                rhs_scale=h_scales[:, cols],
+                start=True,
+                stop=True,
+            )
+            projected[(block, jt)] = bank
 
-        def prepare_v(g, half):
-            words = v_sb[:].bitcast(F32)
+        def finish(block, jt):
+            rows = slice(jt * P, (jt + 1) * P)
+            cols = slice(block * L_BLOCK, (block + 1) * L_BLOCK)
+            result = store.tile([P, L_BLOCK], F32)
+            nc.vector.scalar_tensor_tensor(
+                out=result[:],
+                in0=projected[(block, jt)][:],
+                scalar=bo_col[:, jt : jt + 1],
+                in1=mask_queries[:, cols],
+                op0=ALU.add,
+                op1=ALU.mult,
+            )
+            nc.sync.dma_start(out=out[0, rows, cols], in_=result[:])
+
+        def turn_piece(n):
             turned = psum_turn.tile([P, 2, 2 * P], F32, tag="turn")
             for u in range(2):
                 for s in range(2):
-                    first = g * 2 * P + u * P
-                    nc.tensor.transpose(
-                        turned[:, u, s * P : (s + 1) * P], words[:, 2 * half + s, first : first + P], ident_f32[:]
-                    )
+                    if n < V_PIECES:
+                        first = (n // 2) * 2 * P + u * P
+                        words = v_sb[:].bitcast(F32)[:, 2 * (n % 2) + s, first : first + P]
+                    else:
+                        words = wo_sb[:].bitcast(F32)[:, 2 * (n - V_PIECES) + s, u * P : (u + 1) * P]
+                    nc.tensor.transpose(turned[:, u, s * P : (s + 1) * P], words, ident_f32[:])
+            turned_pieces[n] = turned
+
+        def group_piece(n):
             grouped = work.tile([P, 2 * P, PACK], BF16, align_bytes=64, tag="grouped_w")
-            nc.scalar.copy(
-                out=grouped[:].bitcast(F32).rearrange("p (e r) u -> p e r u", e=2),
-                in_=turned[:].rearrange("p u (r e) -> p e r u", e=2),
-            )
-            cols = slice(half * 2 * P, (half + 1) * 2 * P)
+            if n < V_PIECES:
+                nc.scalar.copy(
+                    out=grouped[:].bitcast(F32).rearrange("p (e r) u -> p e r u", e=2),
+                    in_=turned_pieces[n][:].rearrange("p u (r e) -> p e r u", e=2),
+                )
+            else:
+                nc.vector.tensor_copy(out=grouped[:].bitcast(F32), in_=turned_pieces[n][:].rearrange("p u j -> p j u"))
+            grouped_pieces[n] = grouped
+
+        def quantise_piece(n):
+            if n < V_PIECES:
+                cols = slice((n % 2) * 2 * P, (n % 2 + 1) * 2 * P)
+                codes, scales = v_codes[:, n // 2, cols], v_scales[:, n // 2, cols]
+            else:
+                cols = slice((n - V_PIECES) * 2 * P, (n - V_PIECES + 1) * 2 * P)
+                codes, scales = wo_codes[:, cols], wo_scales[:, cols]
             nc.vector.quantize_mx(
-                out=v_codes[:, g, cols].bitcast(FP8X4),
-                scales=v_scales[:, g, cols],
-                in_=grouped[:].rearrange("p n t -> p (n t)"),
+                out=codes.bitcast(FP8X4), scales=scales, in_=grouped_pieces[n][:].rearrange("p n t -> p (n t)")
             )
 
-        def prepare_wo(pair):
-            words = wo_sb[:].bitcast(F32)
-            turned = psum_turn.tile([P, 2, 2 * P], F32, tag="turn")
-            for u in range(2):
-                for s in range(2):
-                    nc.tensor.transpose(
-                        turned[:, u, s * P : (s + 1) * P], words[:, 2 * pair + s, u * P : (u + 1) * P], ident_f32[:]
-                    )
-            grouped = work.tile([P, 2 * P, PACK], BF16, align_bytes=64, tag="grouped_w")
-            nc.vector.tensor_copy(out=grouped[:].bitcast(F32), in_=turned[:].rearrange("p u j -> p j u"))
-            cols = slice(pair * 2 * P, (pair + 1) * 2 * P)
-            nc.vector.quantize_mx(
-                out=wo_codes[:, cols].bitcast(FP8X4),
-                scales=wo_scales[:, cols],
-                in_=grouped[:].rearrange("p n t -> p (n t)"),
-            )
-
-        def prepare_bias():
+        def turn_bias():
             turned = psum_turn.tile([P, P], BF16, tag="turn")
             nc.tensor.transpose(turned[:], bo_rows[:], ident_bf16[:])
-            nc.vector.tensor_copy(out=bo_col[:], in_=turned[:, 0:J_TILES])
+            turned_pieces["bias"] = turned
 
-        first_project = 5
-        steps = first_project + (L // L_BLOCK) * (J_TILES // J_PER_STEP)
-        energy([0, 1])
+        def copy_bias():
+            nc.vector.tensor_copy(out=bo_col[:], in_=turned_pieces["bias"][:, 0:J_TILES])
+
+        def tile_at(step, stage):
+            i = step - CHAIN.index(stage)
+            return i if 0 <= i < L_TILES else None
+
+        def block_part_at(step, stage):
+            x = step - CHAIN.index(stage) - (TILES_PER_BLOCK - 1)
+            return divmod(x, TILES_PER_BLOCK) if 0 <= x < L_TILES else None
+
+        def piece_at(step, stage_depth):
+            n = step - FIRST_PIECE_STEP - stage_depth
+            return n if 0 <= n < V_PIECES + WO_PIECES else None
+
+        def run(stage_function, item):
+            if item is not None:
+                stage_function(item)
+
+        def run_block(stage_function, block_part):
+            if block_part is not None:
+                block, part = block_part
+                for jt in range(part * J_PER_STEP, (part + 1) * J_PER_STEP):
+                    stage_function(block, jt)
+
+        bias_step = FIRST_PIECE_STEP + V_PIECES + WO_PIECES
+        steps = len(CHAIN) + L_TILES + TILES_PER_BLOCK - 2
+        ctx.enter_context(tc.manual_schedule())
         for step in range(steps):
-            if step < L_TILES:
-                softmax(step)
-            if step + 2 < L_TILES:
-                energy([step + 2])
-            if 0 <= step - 2 < L_TILES:
-                attend(step - 2)
-            if step >= first_project:
-                block, part = divmod(step - first_project, J_TILES // J_PER_STEP)
-                project(block, range(part * J_PER_STEP, (part + 1) * J_PER_STEP))
-            if step < 2:
-                prepare_v(step, 0)
-                prepare_v(step, 1)
-            elif step < 4:
-                prepare_wo(2 * (step - 2))
-                prepare_wo(2 * (step - 2) + 1)
-            elif step == 4:
-                prepare_bias()
-            if 0 <= step - 3 < L_TILES:
-                turn_hidden(step - 3)
-            if 0 <= step - 1 < L_TILES:
-                turn_weights(step - 1)
+            run(scores, tile_at(step, "scores"))
+            run(exponentials, tile_at(step, "exponentials"))
+            run(weigh, tile_at(step, "weigh"))
+            run(quantise_weights, tile_at(step, "quantise_weights"))
+            run(quantise_piece, piece_at(step, 2))
+            run(quantise_hidden, tile_at(step, "quantise_hidden"))
+            run(group_weights, tile_at(step, "group_weights"))
+            run(group_piece, piece_at(step, 1))
+            if step == bias_step + 1:
+                copy_bias()
+            run(energy, tile_at(step, "energy"))
+            run(attend, tile_at(step, "attend"))
+            run(hidden, tile_at(step, "hidden"))
+            run(group_hidden, tile_at(step, "group_hidden"))
+            run_block(project, block_part_at(step, "project"))
+            run_block(finish, block_part_at(step, "finish"))
+            run(turn_weights, tile_at(step, "turn_weights"))
+            run(turn_hidden, tile_at(step, "turn_hidden"))
+            run(turn_piece, piece_at(step, 0))
+            if step == bias_step:
+                turn_bias()

@@ -26,28 +26,10 @@ L_TILES = L // P
 J_TILES = C // P
 KEY_PASSES = L // K_PASS
 L_BLOCK = 256
-TILES_PER_BLOCK = L_BLOCK // P
-J_PER_STEP = J_TILES // TILES_PER_BLOCK
-V_PIECES = 4
-WO_PIECES = 4
-
-CHAIN = [
-    "energy",
-    "scores",
-    "exponentials",
-    "weigh",
-    "turn_weights",
-    "group_weights",
-    "quantise_weights",
-    "attend",
-    "hidden",
-    "turn_hidden",
-    "group_hidden",
-    "quantise_hidden",
-    "project",
-    "finish",
-]
-FIRST_PIECE_STEP = 2
+J_PER_STEP = 4
+ENERGY_AHEAD = 2
+TURN_LAG = 2
+ATTEND_LAG = 5
 
 FLOPS = 2 * L * L * CP + 2 * CP * L * L + 2 * C * CP * L
 
@@ -128,20 +110,13 @@ def tile_attlayer_pa_kernel(tc, q, k, v, mask, wo, bo, out):
         bo_col = keep.tile([P, J_TILES], F32)
 
         energy_banks = {}
-        shifted = {}
-        exponents = {}
-        row_sums = {}
         weights = {}
-        turned_weights = {}
+        row_sums = {}
         grouped_weights = {}
         weight_codes = {}
-        attended = {}
-        hidden_tiles = {}
-        turned_hidden = {}
+        hidden = {}
         grouped_hidden = {}
-        turned_pieces = {}
-        grouped_pieces = {}
-        projected = {}
+        prepared = {}
 
         def energy(i):
             for g in range(KEY_PASSES):
@@ -156,7 +131,7 @@ def tile_attlayer_pa_kernel(tc, q, k, v, mask, wo, bo, out):
                     )
                 energy_banks[(i, g)] = bank
 
-        def scores(i):
+        def softmax(i):
             z = work.tile([P, L], F32)
             for g in range(KEY_PASSES):
                 cols = slice(g * BANK, (g + 1) * BANK)
@@ -170,21 +145,14 @@ def tile_attlayer_pa_kernel(tc, q, k, v, mask, wo, bo, out):
                 )
             neg_max = stats.tile([P, 1], F32)
             nc.vector.tensor_reduce(out=neg_max[:], in_=z[:], axis=mybir.AxisListType.X, op=ALU.max, negate=True)
-            shifted[i] = (z, neg_max)
-
-        def exponentials(i):
-            z, neg_max = shifted[i]
             exp_z = work.tile([P, L], F32)
             row_sum = stats.tile([P, 1], F32)
             nc.scalar.activation(
                 out=exp_z[:], in_=z[:], func=ACT.Exp, bias=neg_max[:, 0:1], scale=1.0, accum_out=row_sum[:, 0:1]
             )
-            exponents[i] = exp_z
             row_sums[i] = row_sum
-
-        def weigh(i):
             p = work.tile([P, L], BF16)
-            nc.gpsimd.tensor_tensor(out=p[:], in0=exponents[i][:], in1=mask_keys[:], op=ALU.mult)
+            nc.gpsimd.tensor_tensor(out=p[:], in0=exp_z[:], in1=mask_keys[:], op=ALU.mult)
             weights[i] = p
 
         def turn_weights(i):
@@ -194,15 +162,8 @@ def tile_attlayer_pa_kernel(tc, q, k, v, mask, wo, bo, out):
                     for e in range(2):
                         first = g * K_PASS + e * 2 * P + u * P
                         nc.tensor.transpose(turned[:, g, 2 * u + e, :], weights[i][:, first : first + P], ident_bf16[:])
-            turned_weights[i] = turned
-
-        def group_weights(i):
             grouped = work.tile([P, KEY_PASSES, P, PACK], BF16, align_bytes=64, tag="grouped_p")
-            values_last = turned_weights[i][:].rearrange("p g t r -> p g r t")
-            if i < L_TILES // 2:
-                nc.scalar.copy(out=grouped[:], in_=values_last)
-            else:
-                nc.vector.tensor_copy(out=grouped[:], in_=values_last)
+            nc.scalar.copy(out=grouped[:], in_=turned[:].rearrange("p g t r -> p g r t"))
             grouped_weights[i] = grouped
 
         def quantise_weights(i):
@@ -217,10 +178,10 @@ def tile_attlayer_pa_kernel(tc, q, k, v, mask, wo, bo, out):
 
         def attend(i):
             codes, scales = weight_codes[i]
-            bank = psum_mx.tile([P, CP], F32, tag="mx")
+            attended = psum_mx.tile([P, CP], F32, tag="mx")
             for g in range(KEY_PASSES):
                 nc.tensor.matmul_mx(
-                    out=bank[:],
+                    out=attended[:],
                     lhsT=codes[:, g, :].bitcast(FP8X4),
                     lhsT_scale=scales[:, g, :],
                     rhs=v_codes[:, g, :].bitcast(FP8X4),
@@ -230,23 +191,16 @@ def tile_attlayer_pa_kernel(tc, q, k, v, mask, wo, bo, out):
                 )
             inv_sum = stats.tile([P, 1], F32)
             nc.vector.reciprocal(out=inv_sum[:], in_=row_sums[i][:])
-            attended[i] = (bank, inv_sum)
-
-        def hidden(i):
-            bank, inv_sum = attended[i]
             h = work.tile([P, CP], BF16)
-            nc.scalar.activation(out=h[:], in_=bank[:], func=ACT.Relu, scale=inv_sum[:, 0:1])
-            hidden_tiles[i] = h
+            nc.scalar.activation(out=h[:], in_=attended[:], func=ACT.Relu, scale=inv_sum[:, 0:1])
+            hidden[i] = h
 
         def turn_hidden(i):
             turned = psum_turn.tile([P, PACK, P], BF16, tag="turn")
             for t in range(PACK):
-                nc.tensor.transpose(turned[:, t, :], hidden_tiles[i][:, t * P : (t + 1) * P], ident_bf16[:])
-            turned_hidden[i] = turned
-
-        def group_hidden(i):
+                nc.tensor.transpose(turned[:, t, :], hidden[i][:, t * P : (t + 1) * P], ident_bf16[:])
             grouped = work.tile([P, P, PACK], BF16, align_bytes=64, tag="grouped_h")
-            nc.scalar.copy(out=grouped[:], in_=turned_hidden[i][:].rearrange("p t r -> p r t"))
+            nc.scalar.copy(out=grouped[:], in_=turned[:].rearrange("p t r -> p r t"))
             grouped_hidden[i] = grouped
 
         def quantise_hidden(i):
@@ -257,121 +211,105 @@ def tile_attlayer_pa_kernel(tc, q, k, v, mask, wo, bo, out):
                 in_=grouped_hidden[i][:].rearrange("p r t -> p (r t)"),
             )
 
-        def project(block, jt):
-            bank = psum_energy.tile([P, L_BLOCK], F32, tag="energy")
-            rows = slice(jt * P, (jt + 1) * P)
+        def project(block, j_tiles):
             cols = slice(block * L_BLOCK, (block + 1) * L_BLOCK)
-            nc.tensor.matmul_mx(
-                out=bank[:],
-                lhsT=wo_codes[:, rows].bitcast(FP8X4),
-                lhsT_scale=wo_scales[:, rows],
-                rhs=h_codes[:, cols].bitcast(FP8X4),
-                rhs_scale=h_scales[:, cols],
-                start=True,
-                stop=True,
-            )
-            projected[(block, jt)] = bank
+            for jt in j_tiles:
+                rows = slice(jt * P, (jt + 1) * P)
+                projected = psum_energy.tile([P, L_BLOCK], F32, tag="energy")
+                nc.tensor.matmul_mx(
+                    out=projected[:],
+                    lhsT=wo_codes[:, rows].bitcast(FP8X4),
+                    lhsT_scale=wo_scales[:, rows],
+                    rhs=h_codes[:, cols].bitcast(FP8X4),
+                    rhs_scale=h_scales[:, cols],
+                    start=True,
+                    stop=True,
+                )
+                result = store.tile([P, L_BLOCK], F32)
+                nc.vector.scalar_tensor_tensor(
+                    out=result[:],
+                    in0=projected[:],
+                    scalar=bo_col[:, jt : jt + 1],
+                    in1=mask_queries[:, cols],
+                    op0=ALU.add,
+                    op1=ALU.mult,
+                )
+                nc.sync.dma_start(out=out[0, rows, cols], in_=result[:])
 
-        def finish(block, jt):
-            rows = slice(jt * P, (jt + 1) * P)
-            cols = slice(block * L_BLOCK, (block + 1) * L_BLOCK)
-            result = store.tile([P, L_BLOCK], F32)
-            nc.vector.scalar_tensor_tensor(
-                out=result[:],
-                in0=projected[(block, jt)][:],
-                scalar=bo_col[:, jt : jt + 1],
-                in1=mask_queries[:, cols],
-                op0=ALU.add,
-                op1=ALU.mult,
-            )
-            nc.sync.dma_start(out=out[0, rows, cols], in_=result[:])
-
-        def turn_piece(n):
+        def prepare_v(step, g, half):
+            words = v_sb[:].bitcast(F32)
             turned = psum_turn.tile([P, 2, 2 * P], F32, tag="turn")
             for u in range(2):
                 for s in range(2):
-                    if n < V_PIECES:
-                        first = (n // 2) * 2 * P + u * P
-                        words = v_sb[:].bitcast(F32)[:, 2 * (n % 2) + s, first : first + P]
-                    else:
-                        words = wo_sb[:].bitcast(F32)[:, 2 * (n - V_PIECES) + s, u * P : (u + 1) * P]
-                    nc.tensor.transpose(turned[:, u, s * P : (s + 1) * P], words, ident_f32[:])
-            turned_pieces[n] = turned
-
-        def group_piece(n):
+                    first = g * 2 * P + u * P
+                    nc.tensor.transpose(
+                        turned[:, u, s * P : (s + 1) * P], words[:, 2 * half + s, first : first + P], ident_f32[:]
+                    )
             grouped = work.tile([P, 2 * P, PACK], BF16, align_bytes=64, tag="grouped_w")
-            if n < V_PIECES:
-                nc.scalar.copy(
-                    out=grouped[:].bitcast(F32).rearrange("p (e r) u -> p e r u", e=2),
-                    in_=turned_pieces[n][:].rearrange("p u (r e) -> p e r u", e=2),
-                )
-            else:
-                nc.vector.tensor_copy(out=grouped[:].bitcast(F32), in_=turned_pieces[n][:].rearrange("p u j -> p j u"))
-            grouped_pieces[n] = grouped
+            nc.scalar.copy(
+                out=grouped[:].bitcast(F32).rearrange("p (e r) u -> p e r u", e=2),
+                in_=turned[:].rearrange("p u (r e) -> p e r u", e=2),
+            )
+            cols = slice(half * 2 * P, (half + 1) * 2 * P)
+            prepared[step] = (grouped, v_codes[:, g, cols], v_scales[:, g, cols])
 
-        def quantise_piece(n):
-            if n < V_PIECES:
-                cols = slice((n % 2) * 2 * P, (n % 2 + 1) * 2 * P)
-                codes, scales = v_codes[:, n // 2, cols], v_scales[:, n // 2, cols]
-            else:
-                cols = slice((n - V_PIECES) * 2 * P, (n - V_PIECES + 1) * 2 * P)
-                codes, scales = wo_codes[:, cols], wo_scales[:, cols]
+        def prepare_wo(step, pair):
+            words = wo_sb[:].bitcast(F32)
+            turned = psum_turn.tile([P, 2, 2 * P], F32, tag="turn")
+            for u in range(2):
+                for s in range(2):
+                    nc.tensor.transpose(
+                        turned[:, u, s * P : (s + 1) * P], words[:, 2 * pair + s, u * P : (u + 1) * P], ident_f32[:]
+                    )
+            grouped = work.tile([P, 2 * P, PACK], BF16, align_bytes=64, tag="grouped_w")
+            nc.scalar.copy(out=grouped[:].bitcast(F32), in_=turned[:].rearrange("p u j -> p j u"))
+            cols = slice(pair * 2 * P, (pair + 1) * 2 * P)
+            prepared[step] = (grouped, wo_codes[:, cols], wo_scales[:, cols])
+
+        def quantise_prepared(step):
+            grouped, codes, scales = prepared[step]
             nc.vector.quantize_mx(
-                out=codes.bitcast(FP8X4), scales=scales, in_=grouped_pieces[n][:].rearrange("p n t -> p (n t)")
+                out=codes.bitcast(FP8X4), scales=scales, in_=grouped[:].rearrange("p n t -> p (n t)")
             )
 
-        def turn_bias():
+        def prepare_bias():
             turned = psum_turn.tile([P, P], BF16, tag="turn")
             nc.tensor.transpose(turned[:], bo_rows[:], ident_bf16[:])
-            turned_pieces["bias"] = turned
+            nc.vector.tensor_copy(out=bo_col[:], in_=turned[:, 0:J_TILES])
 
-        def copy_bias():
-            nc.vector.tensor_copy(out=bo_col[:], in_=turned_pieces["bias"][:, 0:J_TILES])
+        v_pieces = 2 * KEY_PASSES
+        wo_pieces = C // (2 * P)
+        first_project = ATTEND_LAG + 4
+        steps = first_project + (L // L_BLOCK) * (J_TILES // J_PER_STEP)
 
-        def tile_at(step, stage):
-            i = step - CHAIN.index(stage)
-            return i if 0 <= i < L_TILES else None
+        def is_tile(i):
+            return 0 <= i < L_TILES
 
-        def block_part_at(step, stage):
-            x = step - CHAIN.index(stage) - (TILES_PER_BLOCK - 1)
-            return divmod(x, TILES_PER_BLOCK) if 0 <= x < L_TILES else None
-
-        def piece_at(step, stage_depth):
-            n = step - FIRST_PIECE_STEP - stage_depth
-            return n if 0 <= n < V_PIECES + WO_PIECES else None
-
-        def run(stage_function, item):
-            if item is not None:
-                stage_function(item)
-
-        def run_block(stage_function, block_part):
-            if block_part is not None:
-                block, part = block_part
-                for jt in range(part * J_PER_STEP, (part + 1) * J_PER_STEP):
-                    stage_function(block, jt)
-
-        bias_step = FIRST_PIECE_STEP + V_PIECES + WO_PIECES
-        steps = len(CHAIN) + L_TILES + TILES_PER_BLOCK - 2
-        ctx.enter_context(tc.manual_schedule())
+        for i in range(ENERGY_AHEAD):
+            energy(i)
         for step in range(steps):
-            run(scores, tile_at(step, "scores"))
-            run(exponentials, tile_at(step, "exponentials"))
-            run(weigh, tile_at(step, "weigh"))
-            run(quantise_weights, tile_at(step, "quantise_weights"))
-            run(quantise_piece, piece_at(step, 2))
-            run(quantise_hidden, tile_at(step, "quantise_hidden"))
-            run(group_weights, tile_at(step, "group_weights"))
-            run(group_piece, piece_at(step, 1))
-            if step == bias_step + 1:
-                copy_bias()
-            run(energy, tile_at(step, "energy"))
-            run(attend, tile_at(step, "attend"))
-            run(hidden, tile_at(step, "hidden"))
-            run(group_hidden, tile_at(step, "group_hidden"))
-            run_block(project, block_part_at(step, "project"))
-            run_block(finish, block_part_at(step, "finish"))
-            run(turn_weights, tile_at(step, "turn_weights"))
-            run(turn_hidden, tile_at(step, "turn_hidden"))
-            run(turn_piece, piece_at(step, 0))
-            if step == bias_step:
-                turn_bias()
+            if is_tile(step):
+                softmax(step)
+            if is_tile(step - TURN_LAG - 1):
+                quantise_weights(step - TURN_LAG - 1)
+            if 0 <= step - 1 < v_pieces + wo_pieces:
+                quantise_prepared(step - 1)
+            if is_tile(step - ATTEND_LAG - 2):
+                quantise_hidden(step - ATTEND_LAG - 2)
+            if is_tile(step + ENERGY_AHEAD):
+                energy(step + ENERGY_AHEAD)
+            if is_tile(step - ATTEND_LAG):
+                attend(step - ATTEND_LAG)
+            if step >= first_project:
+                block, part = divmod(step - first_project, J_TILES // J_PER_STEP)
+                project(block, range(part * J_PER_STEP, (part + 1) * J_PER_STEP))
+            if is_tile(step - ATTEND_LAG - 1):
+                turn_hidden(step - ATTEND_LAG - 1)
+            if is_tile(step - TURN_LAG):
+                turn_weights(step - TURN_LAG)
+            if step < v_pieces:
+                prepare_v(step, step // 2, step % 2)
+            elif step < v_pieces + wo_pieces:
+                prepare_wo(step, step - v_pieces)
+            elif step == v_pieces + wo_pieces:
+                prepare_bias()

@@ -14,6 +14,7 @@ ACT = mybir.ActivationFunctionType
 
 P = 128
 PACK = 4
+PAIRS = 2
 K_PASS = P * PACK
 BANK = 512
 CP = 512
@@ -26,10 +27,29 @@ L_TILES = L // P
 J_TILES = C // P
 KEY_PASSES = L // K_PASS
 L_BLOCK = 256
-J_PER_STEP = 4
-ENERGY_AHEAD = 2
-TURN_LAG = 2
-ATTEND_LAG = 5
+TILES_PER_BLOCK = L_BLOCK // P
+J_PER_STEP = J_TILES // TILES_PER_BLOCK
+PIECE_ROWS = 256
+V_PIECES = KEY_PASSES * CP // PIECE_ROWS
+WO_PIECES = C // PIECE_ROWS
+
+CHAIN = [
+    "energy",
+    "scores",
+    "exponentials",
+    "weigh",
+    "turn_weights",
+    "group_weights",
+    "quantise_weights",
+    "attend",
+    "hidden",
+    "turn_hidden",
+    "group_hidden",
+    "quantise_hidden",
+    "project",
+    "finish",
+]
+FIRST_PIECE_STEP = 2
 
 FLOPS = 2 * L * L * CP + 2 * CP * L * L + 2 * C * CP * L
 
@@ -80,26 +100,17 @@ def tile_attlayer_pa_kernel(tc, q, k, v, mask, wo, bo, out):
         ident_f32 = keep.tile([P, P], F32)
         make_identity(nc, ident_f32[:])
 
-        mask_queries = keep.tile([P, L], F32)
-        mask_keys = keep.tile([P, L], F32)
-        log_mask_keys = keep.tile([P, L], F32)
-        for g in range(KEY_PASSES):
+        mask_all = keep.tile([P, L], F32)
+        log_mask = keep.tile([P, L], F32)
+        for g in range(L // BANK):
             cols = slice(g * BANK, (g + 1) * BANK)
             spread = psum_mx.tile([P, BANK], F32, tag="mx")
             nc.tensor.matmul(out=spread[:], lhsT=ones[:], rhs=mask_rows[:, cols], start=True, stop=True)
-            in_key_order = spread[:].rearrange("p (w e) -> p e w", e=2)
-            nc.scalar.activation(
-                out=log_mask_keys[:, cols].rearrange("p (e w) -> p e w", e=2),
-                in_=in_key_order,
-                func=ACT.Ln,
-                bias=eps[:, 0:1],
-                scale=1.0,
-            )
-            nc.vector.tensor_copy(out=mask_keys[:, cols].rearrange("p (e w) -> p e w", e=2), in_=in_key_order)
-            nc.vector.tensor_copy(out=mask_queries[:, cols], in_=spread[:])
+            nc.scalar.activation(out=log_mask[:, cols], in_=spread[:], func=ACT.Ln, bias=eps[:, 0:1], scale=1.0)
+            nc.vector.tensor_copy(out=mask_all[:, cols], in_=spread[:])
 
         table_change = keep.tile([P, 1], F32)
-        nc.scalar.activation(out=table_change[:], in_=log_mask_keys[:, L - 1 : L], func=ACT.Exp)
+        nc.scalar.activation(out=table_change[:], in_=log_mask[:, L - 1 : L], func=ACT.Exp)
 
         v_codes = keep.tile([P, KEY_PASSES, CP], U32, align_bytes=64)
         v_scales = keep.tile([P, KEY_PASSES, CP], U8, align_bytes=64)
@@ -110,28 +121,35 @@ def tile_attlayer_pa_kernel(tc, q, k, v, mask, wo, bo, out):
         bo_col = keep.tile([P, J_TILES], F32)
 
         energy_banks = {}
-        weights = {}
+        shifted = {}
+        exponents = {}
         row_sums = {}
+        weights = {}
+        turned_weights = {}
         grouped_weights = {}
         weight_codes = {}
-        hidden = {}
+        attended = {}
+        hidden_tiles = {}
+        turned_hidden = {}
         grouped_hidden = {}
-        prepared = {}
+        turned_pieces = {}
+        grouped_pieces = {}
+        projected = {}
 
         def energy(i):
             for g in range(KEY_PASSES):
                 bank = psum_energy.tile([P, BANK], F32, tag="energy")
                 for ct in range(C_TILES):
                     nc.tensor.matmul(
-                        out=bank[:].rearrange("p (e w) -> p e w", e=2),
+                        out=bank[:],
                         lhsT=queries[i][:, ct, :],
-                        rhs=k_halves[g][:, ct, :].rearrange("p (w e) -> p e w", e=2),
+                        rhs=k_halves[g][:, ct, :],
                         start=(ct == 0),
                         stop=(ct == C_TILES - 1),
                     )
                 energy_banks[(i, g)] = bank
 
-        def softmax(i):
+        def scores(i):
             z = work.tile([P, L], F32)
             for g in range(KEY_PASSES):
                 cols = slice(g * BANK, (g + 1) * BANK)
@@ -139,31 +157,45 @@ def tile_attlayer_pa_kernel(tc, q, k, v, mask, wo, bo, out):
                     out=z[:, cols],
                     in0=energy_banks[(i, g)][:],
                     scalar=1.0 / math.sqrt(CP),
-                    in1=log_mask_keys[:, cols],
+                    in1=log_mask[:, cols],
                     op0=ALU.mult,
                     op1=ALU.add,
                 )
             neg_max = stats.tile([P, 1], F32)
             nc.vector.tensor_reduce(out=neg_max[:], in_=z[:], axis=mybir.AxisListType.X, op=ALU.max, negate=True)
+            shifted[i] = (z, neg_max)
+
+        def exponentials(i):
+            z, neg_max = shifted[i]
             exp_z = work.tile([P, L], F32)
             row_sum = stats.tile([P, 1], F32)
             nc.scalar.activation(
                 out=exp_z[:], in_=z[:], func=ACT.Exp, bias=neg_max[:, 0:1], scale=1.0, accum_out=row_sum[:, 0:1]
             )
+            exponents[i] = exp_z
             row_sums[i] = row_sum
+
+        def weigh(i):
             p = work.tile([P, L], BF16)
-            nc.gpsimd.tensor_tensor(out=p[:], in0=exp_z[:], in1=mask_keys[:], op=ALU.mult)
+            nc.gpsimd.tensor_tensor(out=p[:], in0=exponents[i][:], in1=mask_all[:], op=ALU.mult)
             weights[i] = p
 
         def turn_weights(i):
-            turned = psum_turn.tile([P, KEY_PASSES, PACK, P], BF16, tag="turn")
+            words = weights[i][:].bitcast(F32)
+            turned = psum_turn.tile([P, KEY_PASSES, PAIRS, P], F32, tag="turn")
             for g in range(KEY_PASSES):
-                for u in range(2):
-                    for e in range(2):
-                        first = g * K_PASS + e * 2 * P + u * P
-                        nc.tensor.transpose(turned[:, g, 2 * u + e, :], weights[i][:, first : first + P], ident_bf16[:])
+                for u in range(PAIRS):
+                    first = (g * PAIRS + u) * P
+                    nc.tensor.transpose(turned[:, g, u, :], words[:, first : first + P], ident_f32[:])
+            turned_weights[i] = turned
+
+        def group_weights(i):
             grouped = work.tile([P, KEY_PASSES, P, PACK], BF16, align_bytes=64, tag="grouped_p")
-            nc.scalar.copy(out=grouped[:], in_=turned[:].rearrange("p g t r -> p g r t"))
+            pairs_last = turned_weights[i][:].rearrange("p g u r -> p g r u")
+            if i < L_TILES // 2:
+                nc.scalar.copy(out=grouped[:].bitcast(F32), in_=pairs_last)
+            else:
+                nc.vector.tensor_copy(out=grouped[:].bitcast(F32), in_=pairs_last)
             grouped_weights[i] = grouped
 
         def quantise_weights(i):
@@ -178,10 +210,10 @@ def tile_attlayer_pa_kernel(tc, q, k, v, mask, wo, bo, out):
 
         def attend(i):
             codes, scales = weight_codes[i]
-            attended = psum_mx.tile([P, CP], F32, tag="mx")
+            bank = psum_mx.tile([P, CP], F32, tag="mx")
             for g in range(KEY_PASSES):
                 nc.tensor.matmul_mx(
-                    out=attended[:],
+                    out=bank[:],
                     lhsT=codes[:, g, :].bitcast(FP8X4),
                     lhsT_scale=scales[:, g, :],
                     rhs=v_codes[:, g, :].bitcast(FP8X4),
@@ -191,16 +223,24 @@ def tile_attlayer_pa_kernel(tc, q, k, v, mask, wo, bo, out):
                 )
             inv_sum = stats.tile([P, 1], F32)
             nc.vector.reciprocal(out=inv_sum[:], in_=row_sums[i][:])
+            attended[i] = (bank, inv_sum)
+
+        def hidden(i):
+            bank, inv_sum = attended[i]
             h = work.tile([P, CP], BF16)
-            nc.scalar.activation(out=h[:], in_=attended[:], func=ACT.Relu, scale=inv_sum[:, 0:1])
-            hidden[i] = h
+            nc.scalar.activation(out=h[:], in_=bank[:], func=ACT.Relu, scale=inv_sum[:, 0:1])
+            hidden_tiles[i] = h
 
         def turn_hidden(i):
-            turned = psum_turn.tile([P, PACK, P], BF16, tag="turn")
-            for t in range(PACK):
-                nc.tensor.transpose(turned[:, t, :], hidden[i][:, t * P : (t + 1) * P], ident_bf16[:])
+            words = hidden_tiles[i][:].bitcast(F32)
+            turned = psum_turn.tile([P, PAIRS, P], F32, tag="turn")
+            for u in range(PAIRS):
+                nc.tensor.transpose(turned[:, u, :], words[:, u * P : (u + 1) * P], ident_f32[:])
+            turned_hidden[i] = turned
+
+        def group_hidden(i):
             grouped = work.tile([P, P, PACK], BF16, align_bytes=64, tag="grouped_h")
-            nc.scalar.copy(out=grouped[:], in_=turned[:].rearrange("p t r -> p r t"))
+            nc.scalar.copy(out=grouped[:].bitcast(F32), in_=turned_hidden[i][:].rearrange("p u r -> p r u"))
             grouped_hidden[i] = grouped
 
         def quantise_hidden(i):
@@ -211,105 +251,119 @@ def tile_attlayer_pa_kernel(tc, q, k, v, mask, wo, bo, out):
                 in_=grouped_hidden[i][:].rearrange("p r t -> p (r t)"),
             )
 
-        def project(block, j_tiles):
+        def project(block, jt):
+            bank = psum_energy.tile([P, L_BLOCK], F32, tag="energy")
+            rows = slice(jt * P, (jt + 1) * P)
             cols = slice(block * L_BLOCK, (block + 1) * L_BLOCK)
-            for jt in j_tiles:
-                rows = slice(jt * P, (jt + 1) * P)
-                projected = psum_energy.tile([P, L_BLOCK], F32, tag="energy")
-                nc.tensor.matmul_mx(
-                    out=projected[:],
-                    lhsT=wo_codes[:, rows].bitcast(FP8X4),
-                    lhsT_scale=wo_scales[:, rows],
-                    rhs=h_codes[:, cols].bitcast(FP8X4),
-                    rhs_scale=h_scales[:, cols],
-                    start=True,
-                    stop=True,
-                )
-                result = store.tile([P, L_BLOCK], F32)
-                nc.vector.scalar_tensor_tensor(
-                    out=result[:],
-                    in0=projected[:],
-                    scalar=bo_col[:, jt : jt + 1],
-                    in1=mask_queries[:, cols],
-                    op0=ALU.add,
-                    op1=ALU.mult,
-                )
-                nc.sync.dma_start(out=out[0, rows, cols], in_=result[:])
-
-        def prepare_v(step, g, half):
-            words = v_sb[:].bitcast(F32)
-            turned = psum_turn.tile([P, 2, 2 * P], F32, tag="turn")
-            for u in range(2):
-                for s in range(2):
-                    first = g * 2 * P + u * P
-                    nc.tensor.transpose(
-                        turned[:, u, s * P : (s + 1) * P], words[:, 2 * half + s, first : first + P], ident_f32[:]
-                    )
-            grouped = work.tile([P, 2 * P, PACK], BF16, align_bytes=64, tag="grouped_w")
-            nc.scalar.copy(
-                out=grouped[:].bitcast(F32).rearrange("p (e r) u -> p e r u", e=2),
-                in_=turned[:].rearrange("p u (r e) -> p e r u", e=2),
+            nc.tensor.matmul_mx(
+                out=bank[:],
+                lhsT=wo_codes[:, rows].bitcast(FP8X4),
+                lhsT_scale=wo_scales[:, rows],
+                rhs=h_codes[:, cols].bitcast(FP8X4),
+                rhs_scale=h_scales[:, cols],
+                start=True,
+                stop=True,
             )
-            cols = slice(half * 2 * P, (half + 1) * 2 * P)
-            prepared[step] = (grouped, v_codes[:, g, cols], v_scales[:, g, cols])
+            projected[(block, jt)] = bank
 
-        def prepare_wo(step, pair):
-            words = wo_sb[:].bitcast(F32)
-            turned = psum_turn.tile([P, 2, 2 * P], F32, tag="turn")
-            for u in range(2):
-                for s in range(2):
-                    nc.tensor.transpose(
-                        turned[:, u, s * P : (s + 1) * P], words[:, 2 * pair + s, u * P : (u + 1) * P], ident_f32[:]
-                    )
-            grouped = work.tile([P, 2 * P, PACK], BF16, align_bytes=64, tag="grouped_w")
-            nc.scalar.copy(out=grouped[:].bitcast(F32), in_=turned[:].rearrange("p u j -> p j u"))
-            cols = slice(pair * 2 * P, (pair + 1) * 2 * P)
-            prepared[step] = (grouped, wo_codes[:, cols], wo_scales[:, cols])
+        def finish(block, jt):
+            rows = slice(jt * P, (jt + 1) * P)
+            cols = slice(block * L_BLOCK, (block + 1) * L_BLOCK)
+            result = store.tile([P, L_BLOCK], F32)
+            nc.vector.scalar_tensor_tensor(
+                out=result[:],
+                in0=projected[(block, jt)][:],
+                scalar=bo_col[:, jt : jt + 1],
+                in1=mask_all[:, cols],
+                op0=ALU.add,
+                op1=ALU.mult,
+            )
+            nc.sync.dma_start(out=out[0, rows, cols], in_=result[:])
 
-        def quantise_prepared(step):
-            grouped, codes, scales = prepared[step]
+        def turn_piece(n):
+            turned = psum_turn.tile([P, PAIRS, PIECE_ROWS], F32, tag="turn")
+            for u in range(PAIRS):
+                for s in range(PIECE_ROWS // P):
+                    if n < V_PIECES:
+                        first = ((n // 2) * PAIRS + u) * P
+                        words = v_sb[:].bitcast(F32)[:, 2 * (n % 2) + s, first : first + P]
+                    else:
+                        words = wo_sb[:].bitcast(F32)[:, 2 * (n - V_PIECES) + s, u * P : (u + 1) * P]
+                    nc.tensor.transpose(turned[:, u, s * P : (s + 1) * P], words, ident_f32[:])
+            turned_pieces[n] = turned
+
+        def group_piece(n):
+            grouped = work.tile([P, PIECE_ROWS, PACK], BF16, align_bytes=64, tag="grouped_w")
+            pairs_last = turned_pieces[n][:].rearrange("p u j -> p j u")
+            if n < V_PIECES:
+                nc.scalar.copy(out=grouped[:].bitcast(F32), in_=pairs_last)
+            else:
+                nc.vector.tensor_copy(out=grouped[:].bitcast(F32), in_=pairs_last)
+            grouped_pieces[n] = grouped
+
+        def quantise_piece(n):
+            if n < V_PIECES:
+                cols = slice((n % 2) * PIECE_ROWS, (n % 2 + 1) * PIECE_ROWS)
+                codes, scales = v_codes[:, n // 2, cols], v_scales[:, n // 2, cols]
+            else:
+                cols = slice((n - V_PIECES) * PIECE_ROWS, (n - V_PIECES + 1) * PIECE_ROWS)
+                codes, scales = wo_codes[:, cols], wo_scales[:, cols]
             nc.vector.quantize_mx(
-                out=codes.bitcast(FP8X4), scales=scales, in_=grouped[:].rearrange("p n t -> p (n t)")
+                out=codes.bitcast(FP8X4), scales=scales, in_=grouped_pieces[n][:].rearrange("p n t -> p (n t)")
             )
 
-        def prepare_bias():
+        def turn_bias():
             turned = psum_turn.tile([P, P], BF16, tag="turn")
             nc.tensor.transpose(turned[:], bo_rows[:], ident_bf16[:])
-            nc.vector.tensor_copy(out=bo_col[:], in_=turned[:, 0:J_TILES])
+            turned_pieces["bias"] = turned
 
-        v_pieces = 2 * KEY_PASSES
-        wo_pieces = C // (2 * P)
-        first_project = ATTEND_LAG + 4
-        steps = first_project + (L // L_BLOCK) * (J_TILES // J_PER_STEP)
+        def copy_bias():
+            nc.vector.tensor_copy(out=bo_col[:], in_=turned_pieces["bias"][:, 0:J_TILES])
 
-        def is_tile(i):
-            return 0 <= i < L_TILES
+        def tile_at(step, stage):
+            i = step - CHAIN.index(stage)
+            return i if 0 <= i < L_TILES else None
 
-        for i in range(ENERGY_AHEAD):
-            energy(i)
+        def block_part_at(step, stage):
+            x = step - CHAIN.index(stage) - (TILES_PER_BLOCK - 1)
+            return divmod(x, TILES_PER_BLOCK) if 0 <= x < L_TILES else None
+
+        def piece_at(step, stage_depth):
+            n = step - FIRST_PIECE_STEP - stage_depth
+            return n if 0 <= n < V_PIECES + WO_PIECES else None
+
+        def run(stage_function, item):
+            if item is not None:
+                stage_function(item)
+
+        def run_block(stage_function, block_part):
+            if block_part is not None:
+                block, part = block_part
+                for jt in range(part * J_PER_STEP, (part + 1) * J_PER_STEP):
+                    stage_function(block, jt)
+
+        bias_step = FIRST_PIECE_STEP + V_PIECES + WO_PIECES
+        steps = len(CHAIN) + L_TILES + TILES_PER_BLOCK - 2
+        ctx.enter_context(tc.manual_schedule())
         for step in range(steps):
-            if is_tile(step):
-                softmax(step)
-            if is_tile(step - TURN_LAG - 1):
-                quantise_weights(step - TURN_LAG - 1)
-            if 0 <= step - 1 < v_pieces + wo_pieces:
-                quantise_prepared(step - 1)
-            if is_tile(step - ATTEND_LAG - 2):
-                quantise_hidden(step - ATTEND_LAG - 2)
-            if is_tile(step + ENERGY_AHEAD):
-                energy(step + ENERGY_AHEAD)
-            if is_tile(step - ATTEND_LAG):
-                attend(step - ATTEND_LAG)
-            if step >= first_project:
-                block, part = divmod(step - first_project, J_TILES // J_PER_STEP)
-                project(block, range(part * J_PER_STEP, (part + 1) * J_PER_STEP))
-            if is_tile(step - ATTEND_LAG - 1):
-                turn_hidden(step - ATTEND_LAG - 1)
-            if is_tile(step - TURN_LAG):
-                turn_weights(step - TURN_LAG)
-            if step < v_pieces:
-                prepare_v(step, step // 2, step % 2)
-            elif step < v_pieces + wo_pieces:
-                prepare_wo(step, step - v_pieces)
-            elif step == v_pieces + wo_pieces:
-                prepare_bias()
+            run(scores, tile_at(step, "scores"))
+            run(exponentials, tile_at(step, "exponentials"))
+            run(weigh, tile_at(step, "weigh"))
+            run(quantise_weights, tile_at(step, "quantise_weights"))
+            run(quantise_piece, piece_at(step, 2))
+            run(quantise_hidden, tile_at(step, "quantise_hidden"))
+            run(group_weights, tile_at(step, "group_weights"))
+            run(group_piece, piece_at(step, 1))
+            if step == bias_step + 1:
+                copy_bias()
+            run(energy, tile_at(step, "energy"))
+            run(attend, tile_at(step, "attend"))
+            run(hidden, tile_at(step, "hidden"))
+            run(group_hidden, tile_at(step, "group_hidden"))
+            run_block(project, block_part_at(step, "project"))
+            run_block(finish, block_part_at(step, "finish"))
+            run(turn_weights, tile_at(step, "turn_weights"))
+            run(turn_hidden, tile_at(step, "turn_hidden"))
+            run(turn_piece, piece_at(step, 0))
+            if step == bias_step:
+                turn_bias()

@@ -95,6 +95,8 @@ def tile_attlayer_pa_kernel(tc, q, k, v, mask, wo, bo, out):
         nc.vector.memset(ones[:], 1.0)
         eps = keep.tile([P, 1], F32)
         nc.vector.memset(eps[:], EPS)
+        table_first = keep.tile([P, 1], F32)
+        nc.scalar.activation(out=table_first[:], in_=eps[:], func=ACT.Ln)
         ident_bf16 = keep.tile([P, P], BF16)
         make_identity(nc, ident_bf16[:])
         ident_f32 = keep.tile([P, P], F32)
@@ -121,6 +123,7 @@ def tile_attlayer_pa_kernel(tc, q, k, v, mask, wo, bo, out):
         bo_col = keep.tile([P, J_TILES], F32)
 
         energy_banks = {}
+        masked = {}
         shifted = {}
         exponents = {}
         row_sums = {}
@@ -149,7 +152,7 @@ def tile_attlayer_pa_kernel(tc, q, k, v, mask, wo, bo, out):
                     )
                 energy_banks[(i, g)] = bank
 
-        def scores(i):
+        def add_mask(i):
             z = work.tile([P, L], F32)
             for g in range(KEY_PASSES):
                 cols = slice(g * BANK, (g + 1) * BANK)
@@ -161,9 +164,14 @@ def tile_attlayer_pa_kernel(tc, q, k, v, mask, wo, bo, out):
                     op0=ALU.mult,
                     op1=ALU.add,
                 )
+            masked[i] = z
+
+        def row_max(i):
             neg_max = stats.tile([P, 1], F32)
-            nc.vector.tensor_reduce(out=neg_max[:], in_=z[:], axis=mybir.AxisListType.X, op=ALU.max, negate=True)
-            shifted[i] = (z, neg_max)
+            nc.vector.tensor_reduce(
+                out=neg_max[:], in_=masked[i][:], axis=mybir.AxisListType.X, op=ALU.max, negate=True
+            )
+            shifted[i] = (masked[i], neg_max)
 
         def exponentials(i):
             z, neg_max = shifted[i]
@@ -177,7 +185,9 @@ def tile_attlayer_pa_kernel(tc, q, k, v, mask, wo, bo, out):
 
         def weigh(i):
             p = work.tile([P, L], BF16)
-            nc.gpsimd.tensor_tensor(out=p[:], in0=exponents[i][:], in1=mask_all[:], op=ALU.mult)
+            for g in range(KEY_PASSES):
+                cols = slice(g * K_PASS, (g + 1) * K_PASS)
+                nc.gpsimd.tensor_tensor(out=p[:, cols], in0=exponents[i][:, cols], in1=mask_all[:, cols], op=ALU.mult)
             weights[i] = p
 
         def turn_weights(i):
@@ -346,7 +356,7 @@ def tile_attlayer_pa_kernel(tc, q, k, v, mask, wo, bo, out):
         steps = len(CHAIN) + L_TILES + TILES_PER_BLOCK - 2
         ctx.enter_context(tc.manual_schedule())
         for step in range(steps):
-            run(scores, tile_at(step, "scores"))
+            run(add_mask, tile_at(step, "scores"))
             run(exponentials, tile_at(step, "exponentials"))
             run(weigh, tile_at(step, "weigh"))
             run(quantise_weights, tile_at(step, "quantise_weights"))
@@ -356,6 +366,7 @@ def tile_attlayer_pa_kernel(tc, q, k, v, mask, wo, bo, out):
             run(group_piece, piece_at(step, 1))
             if step == bias_step + 1:
                 copy_bias()
+            run(row_max, tile_at(step, "scores"))
             run(energy, tile_at(step, "energy"))
             run(attend, tile_at(step, "attend"))
             run(hidden, tile_at(step, "hidden"))

@@ -72,20 +72,16 @@ def tile_attlayer_pa_kernel(tc, q, k, v, mask, wo, bo, out):
         nc.vector.memset(bo_rows[:], 0.0)
         nc.scalar.dma_start(out=bo_rows[0:J_TILES, :], in_=bo.rearrange("(t p) -> t p", p=P))
 
-        k_view = k[0].rearrange("(t p) m -> p t m", p=P)
-        q_view = q[0].rearrange("(t p) l -> p t l", p=P)
-        q_first = keep.tile([P, C_TILES, P], BF16)
-        nc.sync.dma_start(out=q_first[:], in_=q_view[:, :, 0:P])
-        k_halves = {}
-        for g in range(KEY_PASSES):
-            k_half = keep.tile([P, C_TILES, BANK], BF16, name="k_half%d" % g)
-            nc.sync.dma_start(out=k_half[:], in_=k_view[:, :, g * BANK : (g + 1) * BANK])
-            k_halves[g] = k_half
-        q_rest = keep.tile([P, C_TILES, L - P], BF16)
-        nc.sync.dma_start(out=q_rest[:], in_=q_view[:, :, P:L])
-        queries = {0: q_first[:]}
-        for i in range(1, L_TILES):
-            queries[i] = q_rest[:, :, (i - 1) * P : i * P]
+        k_tiles = {}
+        q_tiles = {}
+        for ct in range(C_TILES):
+            rows = slice(ct * P, (ct + 1) * P)
+            k_tile = keep.tile([P, L], BF16, name="k_tile%d" % ct)
+            nc.sync.dma_start(out=k_tile[:], in_=k[0, rows, :])
+            k_tiles[ct] = k_tile
+            q_tile = keep.tile([P, L], BF16, name="q_tile%d" % ct)
+            nc.sync.dma_start(out=q_tile[:], in_=q[0, rows, :])
+            q_tiles[ct] = q_tile
         v_sb = keep.tile([P, C_TILES, L], BF16)
         nc.sync.dma_start(out=v_sb[:], in_=v[0].rearrange("(t p) m -> p t m", p=P))
         wo_sb = keep.tile([P, J_TILES, CP], BF16)
@@ -142,15 +138,16 @@ def tile_attlayer_pa_kernel(tc, q, k, v, mask, wo, bo, out):
         def energy(i):
             for g in range(KEY_PASSES):
                 bank = psum_energy.tile([P, BANK], F32, tag="energy")
-                for ct in range(C_TILES):
+                energy_banks[(i, g)] = bank
+            for ct in range(C_TILES):
+                for g in range(KEY_PASSES):
                     nc.tensor.matmul(
-                        out=bank[:],
-                        lhsT=queries[i][:, ct, :],
-                        rhs=k_halves[g][:, ct, :],
+                        out=energy_banks[(i, g)][:],
+                        lhsT=q_tiles[ct][:, i * P : (i + 1) * P],
+                        rhs=k_tiles[ct][:, g * BANK : (g + 1) * BANK],
                         start=(ct == 0),
                         stop=(ct == C_TILES - 1),
                     )
-                energy_banks[(i, g)] = bank
 
         def add_mask(i):
             z = work.tile([P, L], F32)

import math
from contextlib import ExitStack

import concourse.mybir as mybir
from concourse.masks import make_identity

F32 = mybir.dt.float32
BF16 = mybir.dt.bfloat16
U32 = mybir.dt.uint32
U8 = mybir.dt.uint8
FP8X4 = mybir.dt.float8_e4m3fn_x4
ALU = mybir.AluOpType
ACT = mybir.ActivationFunctionType

P = 128
PACK = 4
PAIRS = 2
K_PASS = P * PACK
BANK = 512
CP = 512
L = 1024
C = 1024
EPS = 1e-6

C_TILES = CP // P
L_TILES = L // P
J_TILES = C // P
KEY_PASSES = L // K_PASS
L_BLOCK = 256
TILES_PER_BLOCK = L_BLOCK // P
J_PER_STEP = J_TILES // TILES_PER_BLOCK
PIECE_ROWS = 256
V_PIECES = KEY_PASSES * CP // PIECE_ROWS
WO_PIECES = C // PIECE_ROWS

CHAIN = [
    "energy",
    "scores",
    "exponentials",
    "weigh",
    "turn_weights",
    "group_weights",
    "quantise_weights",
    "attend",
    "hidden",
    "turn_hidden",
    "group_hidden",
    "quantise_hidden",
    "project",
    "finish",
]
FIRST_PIECE_STEP = 2

FLOPS = 2 * L * L * CP + 2 * CP * L * L + 2 * C * CP * L


def tile_attlayer_pa_kernel(tc, q, k, v, mask, wo, bo, out):
    nc = tc.nc
    with ExitStack() as ctx:
        keep = ctx.enter_context(tc.tile_pool(name="keep", bufs=1))
        work = ctx.enter_context(tc.tile_pool(name="work", bufs=4))
        stats = ctx.enter_context(tc.tile_pool(name="stats", bufs=8))
        store = ctx.enter_context(tc.tile_pool(name="store", bufs=8))
        psum_energy = ctx.enter_context(tc.psum_pool(name="psum_energy", bufs=4))
        psum_turn = ctx.enter_context(tc.psum_pool(name="psum_turn", bufs=2))
        psum_mx = ctx.enter_context(tc.psum_pool(name="psum_mx", bufs=2))

        mask_rows = keep.tile([P, L], BF16)
        nc.vector.memset(mask_rows[:], 0.0)
        nc.scalar.dma_start(out=mask_rows[0:1, :], in_=mask[0])
        bo_rows = keep.tile([P, P], BF16)
        nc.vector.memset(bo_rows[:], 0.0)
        nc.scalar.dma_start(out=bo_rows[0:J_TILES, :], in_=bo.rearrange("(t p) -> t p", p=P))

        k_tiles = {}
        q_tiles = {}
        for ct in range(C_TILES):
            rows = slice(ct * P, (ct + 1) * P)
            k_tile = keep.tile([P, L], BF16, name="k_tile%d" % ct)
            nc.sync.dma_start(out=k_tile[:], in_=k[0, rows, :])
            k_tiles[ct] = k_tile
            q_tile = keep.tile([P, L], BF16, name="q_tile%d" % ct)
            nc.sync.dma_start(out=q_tile[:], in_=q[0, rows, :])
            q_tiles[ct] = q_tile
        v_sb = keep.tile([P, C_TILES, L], BF16)
        nc.sync.dma_start(out=v_sb[:], in_=v[0].rearrange("(t p) m -> p t m", p=P))
        wo_sb = keep.tile([P, J_TILES, CP], BF16)
        nc.sync.dma_start(out=wo_sb[:], in_=wo.rearrange("(t p) c -> p t c", p=P))

        ones = keep.tile([P, P], BF16)
        nc.vector.memset(ones[:], 1.0)
        eps = keep.tile([P, 1], F32)
        nc.vector.memset(eps[:], EPS)
        table_first = keep.tile([P, 1], F32)
        nc.scalar.activation(out=table_first[:], in_=eps[:], func=ACT.Ln)
        ident_bf16 = keep.tile([P, P], BF16)
        make_identity(nc, ident_bf16[:])
        ident_f32 = keep.tile([P, P], F32)
        make_identity(nc, ident_f32[:])

        mask_all = keep.tile([P, L], F32)
        log_mask = keep.tile([P, L], F32)
        for g in range(L // BANK):
            cols = slice(g * BANK, (g + 1) * BANK)
            spread = psum_mx.tile([P, BANK], F32, tag="mx")
            nc.tensor.matmul(out=spread[:], lhsT=ones[:], rhs=mask_rows[:, cols], start=True, stop=True)
            nc.scalar.activation(out=log_mask[:, cols], in_=spread[:], func=ACT.Ln, bias=eps[:, 0:1], scale=1.0)
            nc.vector.tensor_copy(out=mask_all[:, cols], in_=spread[:])

        table_change = keep.tile([P, 1], F32)
        nc.scalar.activation(out=table_change[:], in_=log_mask[:, L - 1 : L], func=ACT.Exp)

        v_codes = keep.tile([P, KEY_PASSES, CP], U32, align_bytes=64)
        v_scales = keep.tile([P, KEY_PASSES, CP], U8, align_bytes=64)
        wo_codes = keep.tile([P, C], U32, align_bytes=64)
        wo_scales = keep.tile([P, C], U8, align_bytes=64)
        h_codes = keep.tile([P, L], U32, align_bytes=64)
        h_scales = keep.tile([P, L], U8, align_bytes=64)
        bo_col = keep.tile([P, J_TILES], F32)

        energy_banks = {}
        masked = {}
        shifted = {}
        exponents = {}
        row_sums = {}
        weights = {}
        turned_weights = {}
        grouped_weights = {}
        weight_codes = {}
        attended = {}
        hidden_tiles = {}
        turned_hidden = {}
        grouped_hidden = {}
        turned_pieces = {}
        grouped_pieces = {}
        projected = {}

        def energy(i):
            for g in range(KEY_PASSES):
                bank = psum_energy.tile([P, BANK], F32, tag="energy")
                energy_banks[(i, g)] = bank
            for ct in range(C_TILES):
                for g in range(KEY_PASSES):
                    nc.tensor.matmul(
                        out=energy_banks[(i, g)][:],
                        lhsT=q_tiles[ct][:, i * P : (i + 1) * P],
                        rhs=k_tiles[ct][:, g * BANK : (g + 1) * BANK],
                        start=(ct == 0),
                        stop=(ct == C_TILES - 1),
                    )

        def add_mask(i):
            z = work.tile([P, L], F32)
            for g in range(KEY_PASSES):
                cols = slice(g * BANK, (g + 1) * BANK)
                nc.vector.scalar_tensor_tensor(
                    out=z[:, cols],
                    in0=energy_banks[(i, g)][:],
                    scalar=1.0 / math.sqrt(CP),
                    in1=log_mask[:, cols],
                    op0=ALU.mult,
                    op1=ALU.add,
                )
            masked[i] = z

        def row_max(i):
            neg_max = stats.tile([P, 1], F32)
            nc.vector.tensor_reduce(
                out=neg_max[:], in_=masked[i][:], axis=mybir.AxisListType.X, op=ALU.max, negate=True
            )
            shifted[i] = (masked[i], neg_max)

        def exponentials(i):
            z, neg_max = shifted[i]
            exp_z = work.tile([P, L], F32)
            row_sum = stats.tile([P, 1], F32)
            nc.scalar.activation(
                out=exp_z[:], in_=z[:], func=ACT.Exp, bias=neg_max[:, 0:1], scale=1.0, accum_out=row_sum[:, 0:1]
            )
            exponents[i] = exp_z
            row_sums[i] = row_sum

        def weigh(i):
            p = work.tile([P, L], BF16)
            for g in range(KEY_PASSES):
                cols = slice(g * K_PASS, (g + 1) * K_PASS)
                nc.gpsimd.tensor_tensor(out=p[:, cols], in0=exponents[i][:, cols], in1=mask_all[:, cols], op=ALU.mult)
            weights[i] = p

        def turn_weights(i):
            words = weights[i][:].bitcast(F32)
            turned = psum_turn.tile([P, KEY_PASSES, PAIRS, P], F32, tag="turn")
            for g in range(KEY_PASSES):
                for u in range(PAIRS):
                    first = (g * PAIRS + u) * P
                    nc.tensor.transpose(turned[:, g, u, :], words[:, first : first + P], ident_f32[:])
            turned_weights[i] = turned

        def group_weights(i):
            grouped = work.tile([P, KEY_PASSES, P, PACK], BF16, align_bytes=64, tag="grouped_p")
            pairs_last = turned_weights[i][:].rearrange("p g u r -> p g r u")
            if i < L_TILES // 2:
                nc.scalar.copy(out=grouped[:].bitcast(F32), in_=pairs_last)
            else:
                nc.vector.tensor_copy(out=grouped[:].bitcast(F32), in_=pairs_last)
            grouped_weights[i] = grouped

        def quantise_weights(i):
            codes = work.tile([P, KEY_PASSES, P], U32, align_bytes=64, tag="p_codes")
            scales = work.tile([P, KEY_PASSES, P], U8, align_bytes=64, tag="p_scales")
            nc.vector.quantize_mx(
                out=codes[:].rearrange("p g r -> p (g r)").bitcast(FP8X4),
                scales=scales[:].rearrange("p g r -> p (g r)"),
                in_=grouped_weights[i][:].rearrange("p g r t -> p (g r t)"),
            )
            weight_codes[i] = (codes, scales)

        def attend(i):
            codes, scales = weight_codes[i]
            bank = psum_mx.tile([P, CP], F32, tag="mx")
            for g in range(KEY_PASSES):
                nc.tensor.matmul_mx(
                    out=bank[:],
                    lhsT=codes[:, g, :].bitcast(FP8X4),
                    lhsT_scale=scales[:, g, :],
                    rhs=v_codes[:, g, :].bitcast(FP8X4),
                    rhs_scale=v_scales[:, g, :],
                    start=(g == 0),
                    stop=(g == KEY_PASSES - 1),
                )
            inv_sum = stats.tile([P, 1], F32)
            nc.vector.reciprocal(out=inv_sum[:], in_=row_sums[i][:])
            attended[i] = (bank, inv_sum)

        def hidden(i):
            bank, inv_sum = attended[i]
            h = work.tile([P, CP], BF16)
            nc.scalar.activation(out=h[:], in_=bank[:], func=ACT.Relu, scale=inv_sum[:, 0:1])
            hidden_tiles[i] = h

        def turn_hidden(i):
            words = hidden_tiles[i][:].bitcast(F32)
            turned = psum_turn.tile([P, PAIRS, P], F32, tag="turn")
            for u in range(PAIRS):
                nc.tensor.transpose(turned[:, u, :], words[:, u * P : (u + 1) * P], ident_f32[:])
            turned_hidden[i] = turned

        def group_hidden(i):
            grouped = work.tile([P, P, PACK], BF16, align_bytes=64, tag="grouped_h")
            nc.scalar.copy(out=grouped[:].bitcast(F32), in_=turned_hidden[i][:].rearrange("p u r -> p r u"))
            grouped_hidden[i] = grouped

        def quantise_hidden(i):
            cols = slice(i * P, (i + 1) * P)
            nc.vector.quantize_mx(
                out=h_codes[:, cols].bitcast(FP8X4),
                scales=h_scales[:, cols],
                in_=grouped_hidden[i][:].rearrange("p r t -> p (r t)"),
            )

        def project(block, jt):
            bank = psum_energy.tile([P, L_BLOCK], F32, tag="energy")
            rows = slice(jt * P, (jt + 1) * P)
            cols = slice(block * L_BLOCK, (block + 1) * L_BLOCK)
            nc.tensor.matmul_mx(
                out=bank[:],
                lhsT=wo_codes[:, rows].bitcast(FP8X4),
                lhsT_scale=wo_scales[:, rows],
                rhs=h_codes[:, cols].bitcast(FP8X4),
                rhs_scale=h_scales[:, cols],
                start=True,
                stop=True,
            )
            projected[(block, jt)] = bank

        def finish(block, jt):
            rows = slice(jt * P, (jt + 1) * P)
            cols = slice(block * L_BLOCK, (block + 1) * L_BLOCK)
            result = store.tile([P, L_BLOCK], F32)
            nc.vector.scalar_tensor_tensor(
                out=result[:],
                in0=projected[(block, jt)][:],
                scalar=bo_col[:, jt : jt + 1],
                in1=mask_all[:, cols],
                op0=ALU.add,
                op1=ALU.mult,
            )
            nc.sync.dma_start(out=out[0, rows, cols], in_=result[:])

        def turn_piece(n):
            turned = psum_turn.tile([P, PAIRS, PIECE_ROWS], F32, tag="turn")
            for u in range(PAIRS):
                for s in range(PIECE_ROWS // P):
                    if n < V_PIECES:
                        first = ((n // 2) * PAIRS + u) * P
                        words = v_sb[:].bitcast(F32)[:, 2 * (n % 2) + s, first : first + P]
                    else:
                        words = wo_sb[:].bitcast(F32)[:, 2 * (n - V_PIECES) + s, u * P : (u + 1) * P]
                    nc.tensor.transpose(turned[:, u, s * P : (s + 1) * P], words, ident_f32[:])
            turned_pieces[n] = turned

        def group_piece(n):
            grouped = work.tile([P, PIECE_ROWS, PACK], BF16, align_bytes=64, tag="grouped_w")
            pairs_last = turned_pieces[n][:].rearrange("p u j -> p j u")
            if n < V_PIECES:
                nc.scalar.copy(out=grouped[:].bitcast(F32), in_=pairs_last)
            else:
                nc.vector.tensor_copy(out=grouped[:].bitcast(F32), in_=pairs_last)
            grouped_pieces[n] = grouped

        def quantise_piece(n):
            if n < V_PIECES:
                cols = slice((n % 2) * PIECE_ROWS, (n % 2 + 1) * PIECE_ROWS)
                codes, scales = v_codes[:, n // 2, cols], v_scales[:, n // 2, cols]
            else:
                cols = slice((n - V_PIECES) * PIECE_ROWS, (n - V_PIECES + 1) * PIECE_ROWS)
                codes, scales = wo_codes[:, cols], wo_scales[:, cols]
            nc.vector.quantize_mx(
                out=codes.bitcast(FP8X4), scales=scales, in_=grouped_pieces[n][:].rearrange("p n t -> p (n t)")
            )

        def turn_bias():
            turned = psum_turn.tile([P, P], BF16, tag="turn")
            nc.tensor.transpose(turned[:], bo_rows[:], ident_bf16[:])
            turned_pieces["bias"] = turned

        def copy_bias():
            nc.vector.tensor_copy(out=bo_col[:], in_=turned_pieces["bias"][:, 0:J_TILES])

        def tile_at(step, stage):
            i = step - CHAIN.index(stage)
            return i if 0 <= i < L_TILES else None

        def block_part_at(step, stage):
            x = step - CHAIN.index(stage) - (TILES_PER_BLOCK - 1)
            return divmod(x, TILES_PER_BLOCK) if 0 <= x < L_TILES else None

        def piece_at(step, stage_depth):
            n = step - FIRST_PIECE_STEP - stage_depth
            return n if 0 <= n < V_PIECES + WO_PIECES else None

        def run(stage_function, item):
            if item is not None:
                stage_function(item)

        def run_block(stage_function, block_part):
            if block_part is not None:
                block, part = block_part
                for jt in range(part * J_PER_STEP, (part + 1) * J_PER_STEP):
                    stage_function(block, jt)

        bias_step = FIRST_PIECE_STEP + V_PIECES + WO_PIECES
        steps = len(CHAIN) + L_TILES + TILES_PER_BLOCK - 2
        ctx.enter_context(tc.manual_schedule())
        for step in range(steps):
            run(add_mask, tile_at(step, "scores"))
            run(exponentials, tile_at(step, "exponentials"))
            run(weigh, tile_at(step, "weigh"))
            run(quantise_weights, tile_at(step, "quantise_weights"))
            run(quantise_piece, piece_at(step, 2))
            run(quantise_hidden, tile_at(step, "quantise_hidden"))
            run(group_weights, tile_at(step, "group_weights"))
            run(group_piece, piece_at(step, 1))
            if step == bias_step + 1:
                copy_bias()
            run(row_max, tile_at(step, "scores"))
            run(energy, tile_at(step, "energy"))
            run(attend, tile_at(step, "attend"))
            run(hidden, tile_at(step, "hidden"))
            run(group_hidden, tile_at(step, "group_hidden"))
            run_block(project, block_part_at(step, "project"))
            run_block(finish, block_part_at(step, "finish"))
            run(turn_weights, tile_at(step, "turn_weights"))
            run(turn_hidden, tile_at(step, "turn_hidden"))
            run(turn_piece, piece_at(step, 0))
            if step == bias_step:
                turn_bias()
